import numpy as np
import ml_dtypes


def mxq(x, axis, fmt="e4m3"):
    dtype, down = {"e4m3": (ml_dtypes.float8_e4m3fn, 7), "e5m2": (ml_dtypes.float8_e5m2, 14)}[fmt]
    v = np.moveaxis(np.asarray(x, np.float32).astype(ml_dtypes.bfloat16).astype(np.float64), axis, -1)
    blocks = v.reshape(v.shape[:-1] + (-1, 32))
    amax = np.abs(blocks).max(-1, keepdims=True)
    byte = np.maximum(np.where(amax > 0, np.frexp(amax)[1] - 1 + 127, 0) - down, 1)
    scale = np.exp2(byte - 127.0)
    codes = (blocks / scale).astype(np.float32).astype(dtype).astype(np.float64)
    return np.moveaxis((codes * scale).reshape(v.shape), -1, axis)


WIDE = False


def mx_kscale(k):
    if not WIDE:
        return np.ones(k)
    levels = np.array([10, -10, 5, -5, 0])
    a = np.random.permutation(np.resize(levels, k // 512 * 4)).reshape(k // 512, 4)
    idx = np.arange(k)
    return np.exp2(a[idx // 512, idx % 128 // 32])


BF16 = ml_dtypes.bfloat16


def bf(x):
    return np.asarray(x, np.float32).astype(BF16)


def f64(x):
    return np.asarray(x).astype(np.float64)


B, D_IN, D_H, D_OUT = 512, 1024, 4096, 1024


def setup_inputs():
    s, t = mx_kscale(D_IN), mx_kscale(D_H)
    return {"x": bf(np.random.standard_normal((B, D_IN)) * s),
            "w1": bf(np.random.standard_normal((D_H, D_IN)) * 0.03 / s[None, :] * t[:, None]),
            "w2": bf(np.random.standard_normal((D_OUT, D_H)) * 0.03 / t[None, :])}


def reference(x, w1, w2):
    h = mxq(f64(x), 1, "e4m3") @ mxq(f64(w1), 1, "e4m3").T
    h = np.where(h > 0, h, 0.0)
    return mxq(h, 1, "e4m3") @ mxq(f64(w2), 1, "e4m3").T

@@ -1,0 +1,227 @@
+from contextlib import ExitStack
+
+import concourse.mybir as mybir
+from concourse.masks import make_identity
+
+F32 = mybir.dt.float32
+BF16 = mybir.dt.bfloat16
+U32 = mybir.dt.uint32
+U8 = mybir.dt.uint8
+FP8X4 = mybir.dt.float8_e4m3fn_x4
+RELU = mybir.ActivationFunctionType.Relu
+
+P = 128
+B, D_IN, D_H, D_OUT = 512, 1024, 4096, 1024
+FLOPS = 2 * B * D_IN * D_H + 2 * B * D_H * D_OUT
+
+G = D_H // 512
+Q = D_OUT // 256
+RAW_BUFS = 8
+
+
+def tile_snn_mlp_kernel(tc, x, w1, w2, out):
+    nc = tc.nc
+    with ExitStack() as ctx:
+        const = ctx.enter_context(tc.tile_pool(name="const", bufs=1))
+        rawp = ctx.enter_context(tc.tile_pool(name="rawp", bufs=1))
+        stage = ctx.enter_context(tc.tile_pool(name="stage", bufs=2))
+        psum = ctx.enter_context(tc.psum_pool(name="psum", bufs=1))
+        ctx.enter_context(tc.manual_schedule())
+
+        w1_v = w1.rearrange("(g j p e) k -> g p j e k", g=G, j=2, p=P, e=2)
+        w2_v = w2.rearrange("(i p) k -> i p k", p=P)
+
+        raw = {}
+
+        def load_raw(n):
+            t = rawp.tile([P, 4096], BF16, name="raw%d" % n, tag="slot%d" % (n % RAW_BUFS))
+            raw[n] = t
+            if n == 0:
+                tv = t[:].rearrange("p (j e k) -> p j e k", j=2, e=2)
+                for j in range(2):
+                    nc.sync.dma_start(out=tv[:, j], in_=w1_v[0][:, j])
+            elif n < G:
+                nc.sync.dma_start(out=t[:].rearrange("p (j e k) -> p j e k", j=2, e=2), in_=w1_v[n])
+            else:
+                nc.sync.dma_start(out=t[:], in_=w2_v[n - G])
+
+        def free_raw(n):
+            if n + RAW_BUFS < 2 * G:
+                load_raw(n + RAW_BUFS)
+
+        load_raw(0)
+        xr = []
+        for i in range(4):
+            t = const.tile([P, D_IN], BF16, name="xr%d" % i)
+            nc.sync.dma_start(out=t[:], in_=x[i * P : (i + 1) * P, :])
+            xr.append(t)
+        for n in range(1, RAW_BUFS):
+            load_raw(n)
+
+        ident = const.tile([P, P], F32, name="ident")
+        make_identity(nc, ident[:])
+
+        scr_a = const.tile([P, 1], F32, name="scr_a")
+        scr_b = const.tile([P, 1], F32, name="scr_b")
+        nc.vector.memset(scr_a[:], 0.0)
+        nc.scalar.activation(out=scr_b[:], in_=scr_a[:], func=RELU)
+
+        gx = const.tile([P, 4096], BF16, name="gx", align_bytes=64)
+        xq = const.tile([P, 1024], U32, name="xq", align_bytes=64)
+        xs = const.tile([P, 1024], U8, name="xs", align_bytes=64)
+        hq = const.tile([P, G * 512], U32, name="hq", align_bytes=64)
+        hs = const.tile([P, G * 512], U8, name="hs", align_bytes=64)
+
+        ring = {"tags": ["tp0", "tp1", "tp2", "tp3"], "n": 0}
+
+        def fill(srcs, dst_words, eng):
+            tag = ring["tags"][ring["n"] % len(ring["tags"])]
+            ring["n"] += 1
+            pt = psum.tile([P, 2, 2, P], F32, name="pt", tag=tag)
+            for k in range(4):
+                nc.tensor.transpose(pt[:, k // 2, k % 2, :], srcs[k], ident[:])
+            d = dst_words.rearrange("p (s r u) -> p s r u", s=2, u=2)
+            s = pt[:].rearrange("p s u r -> p s r u")
+            if eng == "v":
+                nc.vector.tensor_copy(out=d, in_=s)
+            else:
+                nc.scalar.copy(out=d, in_=s)
+
+        def quant(codes, scales, src):
+            nc.vector.quantize_mx(out=codes.bitcast(FP8X4), scales=scales, in_=src)
+
+        gx_w = gx[:].bitcast(F32)
+
+        def tx(i):
+            xw = xr[i][:].bitcast(F32)
+            srcs = [xw[:, 256 * c + 128 * u : 256 * c + 128 * u + 128] for c in range(2) for u in range(2)]
+            fill(srcs, gx_w[:, i * 512 : (i + 1) * 512], "av"[i % 2])
+
+        def qx(i):
+            quant(xq[:, i * 256 : (i + 1) * 256], xs[:, i * 256 : (i + 1) * 256], gx[:, i * 1024 : (i + 1) * 1024])
+
+        w1c = {}
+
+        def t1(g):
+            gw = stage.tile([P, 4096], BF16, name="gw1", align_bytes=64, bufs=3)
+            cq = stage.tile([P, 1024], U32, name="w1q", align_bytes=64, bufs=3)
+            cs = stage.tile([P, 1024], U8, name="w1s", align_bytes=64, bufs=3)
+            w1c[g] = (gw, cq, cs)
+            rw = raw[g][:].bitcast(F32)
+            gw_w = gw[:].bitcast(F32)
+            for j in range(2):
+                for c in range(2):
+                    srcs = [
+                        rw[:, j * 1024 + e * 512 + 256 * c + 128 * u : j * 1024 + e * 512 + 256 * c + 128 * u + 128]
+                        for e in range(2)
+                        for u in range(2)
+                    ]
+                    k = j * 2 + c
+                    fill(srcs, gw_w[:, k * 512 : (k + 1) * 512], "av"[c])
+            free_raw(g)
+
+        def q1(g):
+            gw, cq, cs = w1c[g]
+            for j in range(2):
+                quant(cq[:, j * 512 : (j + 1) * 512], cs[:, j * 512 : (j + 1) * 512], gw[:, j * 2048 : (j + 1) * 2048])
+
+        gh = {}
+
+        def m1(g):
+            gw, cq, cs = w1c[g]
+            gt = stage.tile([P, 2048], BF16, name="gh", align_bytes=64, bufs=3)
+            gh[g] = gt
+            for bc in range(4):
+                hp = psum.tile([P, 4, P], F32, name="hp", tag="mp%d" % bc)
+                for t in range(4):
+                    for c in range(2):
+                        lo = (t // 2) * 512 + c * 256 + (t % 2) * 128
+                        ro = bc * 256 + c * 128
+                        nc.tensor.matmul_mx(
+                            out=hp[:, t, :],
+                            lhsT=cq[:, lo : lo + 128].bitcast(FP8X4),
+                            lhsT_scale=cs[:, lo : lo + 128],
+                            rhs=xq[:, ro : ro + 128].bitcast(FP8X4),
+                            rhs_scale=xs[:, ro : ro + 128],
+                            start=(c == 0),
+                            stop=(c == 1),
+                        )
+                d = gt[:, bc * 512 : (bc + 1) * 512].rearrange("p (b t) -> p b t", t=4)
+                s = hp[:].rearrange("p t b -> p b t")
+                nc.scalar.activation(out=d, in_=s, func=RELU)
+
+        def qh(g):
+            quant(hq[:, g * 512 : (g + 1) * 512], hs[:, g * 512 : (g + 1) * 512], gh[g][:])
+
+        w2c = {}
+
+        def t2(q, g_lo, g_hi):
+            if g_lo == 0:
+                gw = stage.tile([P, 8192], BF16, name="gw2", align_bytes=64)
+                cq = stage.tile([P, 2048], U32, name="w2q", align_bytes=64)
+                cs = stage.tile([P, 2048], U8, name="w2s", align_bytes=64)
+                w2c[q] = (gw, cq, cs)
+            gw_w = w2c[q][0][:].bitcast(F32)
+            for g in range(g_lo, g_hi):
+                srcs = [
+                    raw[G + 2 * q + s][:].bitcast(F32)[:, 256 * g + 128 * u : 256 * g + 128 * u + 128]
+                    for s in range(2)
+                    for u in range(2)
+                ]
+                fill(srcs, gw_w[:, g * 512 : (g + 1) * 512], "av"[g % 2])
+            if g_hi == G:
+                free_raw(G + 2 * q)
+                free_raw(G + 2 * q + 1)
+
+        def q2(q, k_lo, k_hi):
+            gw, cq, cs = w2c[q]
+            for k in range(k_lo, k_hi):
+                quant(cq[:, k * 512 : (k + 1) * 512], cs[:, k * 512 : (k + 1) * 512], gw[:, k * 2048 : (k + 1) * 2048])
+
+        def m2(q):
+            gw, cq, cs = w2c[q]
+            banks = [psum.tile([P, 2, 256], F32, name="po%d" % k, tag="mp%d" % k) for k in range(2)]
+            for bt in range(4):
+                po = banks[bt % 2][:, bt // 2, :]
+                for g in range(G):
+                    lo = g * 512 + bt * 128
+                    nc.tensor.matmul_mx(
+                        out=po,
+                        lhsT=hq[:, lo : lo + 128].bitcast(FP8X4),
+                        lhsT_scale=hs[:, lo : lo + 128],
+                        rhs=cq[:, g * 256 : (g + 1) * 256].bitcast(FP8X4),
+                        rhs_scale=cs[:, g * 256 : (g + 1) * 256],
+                        start=(g == 0),
+                        stop=(g == G - 1),
+                    )
+                ot = stage.tile([P, 256], F32, name="ot", bufs=4)
+                if q == Q - 1 and bt % 2 == 1:
+                    nc.vector.tensor_copy(out=ot[:], in_=po)
+                else:
+                    nc.scalar.copy(out=ot[:], in_=po)
+                nc.sync.dma_start(out=out[bt * P : (bt + 1) * P, q * 256 : (q + 1) * 256], in_=ot[:])
+
+        t1(0)
+        q1(0)
+        for i in range(4):
+            tx(i)
+            qx(i)
+        m1(0)
+        t1(1)
+        q1(1)
+        for g in range(1, G):
+            qh(g - 1)
+            if g + 1 < G:
+                t1(g + 1)
+                q1(g + 1)
+            else:
+                t2(0, 0, G)
+                q2(0, 0, 4)
+            m1(g)
+        ring["tags"] = ["tp0", "tp1", "tp2", "tp3", "mp2", "mp3"]
+        qh(G - 1)
+        for q in range(Q):
+            if q + 1 < Q:
+                t2(q + 1, 0, G)
+                q2(q + 1, 0, 4)
+            m2(q)

@@ -95,7 +95,7 @@ def tile_snn_mlp_kernel(tc, x, w1, w2, out):
         def tx(i):
             xw = xr[i][:].bitcast(F32)
             srcs = [xw[:, 256 * c + 128 * u : 256 * c + 128 * u + 128] for c in range(2) for u in range(2)]
-            fill(srcs, gx_w[:, i * 512 : (i + 1) * 512], "av"[i % 2])
+            fill(srcs, gx_w[:, i * 512 : (i + 1) * 512], "a")
 
         def qx(i):
             quant(xq[:, i * 256 : (i + 1) * 256], xs[:, i * 256 : (i + 1) * 256], gx[:, i * 1024 : (i + 1) * 1024])
@@ -118,12 +118,17 @@ def tile_snn_mlp_kernel(tc, x, w1, w2, out):
                     ]
                     k = j * 2 + c
                     fill(srcs, gw_w[:, k * 512 : (k + 1) * 512], "av"[c])
+                if g == 0:
+                    q1j(g, j)
             free_raw(g)
 
-        def q1(g):
+        def q1j(g, j):
             gw, cq, cs = w1c[g]
+            quant(cq[:, j * 512 : (j + 1) * 512], cs[:, j * 512 : (j + 1) * 512], gw[:, j * 2048 : (j + 1) * 2048])
+
+        def q1(g):
             for j in range(2):
-                quant(cq[:, j * 512 : (j + 1) * 512], cs[:, j * 512 : (j + 1) * 512], gw[:, j * 2048 : (j + 1) * 2048])
+                q1j(g, j)
 
         gh = {}
 
@@ -148,7 +153,10 @@ def tile_snn_mlp_kernel(tc, x, w1, w2, out):
                         )
                 d = gt[:, bc * 512 : (bc + 1) * 512].rearrange("p (b t) -> p b t", t=4)
                 s = hp[:].rearrange("p t b -> p b t")
-                nc.scalar.activation(out=d, in_=s, func=RELU)
+                if bc == 3 and g % 2 == 0:
+                    nc.vector.tensor_scalar_max(out=d, in0=s, scalar1=0.0)
+                else:
+                    nc.scalar.activation(out=d, in_=s, func=RELU)
 
         def qh(g):
             quant(hq[:, g * 512 : (g + 1) * 512], hs[:, g * 512 : (g + 1) * 512], gh[g][:])
@@ -202,7 +210,6 @@ def tile_snn_mlp_kernel(tc, x, w1, w2, out):
                 nc.sync.dma_start(out=out[bt * P : (bt + 1) * P, q * 256 : (q + 1) * 256], in_=ot[:])
 
         t1(0)
-        q1(0)
         for i in range(4):
             tx(i)
             qx(i)

@@ -17,6 +17,10 @@ FLOPS = 2 * B * D_IN * D_H + 2 * B * D_H * D_OUT
 G = D_H // 512
 Q = D_OUT // 256
 RAW_BUFS = 8
+WARM_START = 10
+WARM_W1 = (1, 0)
+WARM_X = (1, 0, 1, 1)
+WARM_T1 = (1, 1)
 
 
 def tile_snn_mlp_kernel(tc, x, w1, w2, out):
@@ -66,6 +70,18 @@ def tile_snn_mlp_kernel(tc, x, w1, w2, out):
         nc.vector.memset(scr_a[:], 0.0)
         nc.scalar.activation(out=scr_b[:], in_=scr_a[:], func=RELU)
 
+        wz = const.tile([P, 512], BF16, name="wz")
+        nc.vector.memset(wz[:], 0.0)
+        pend = {"n": 0}
+
+        def warm(n):
+            pend["n"] += n
+
+        def warm_into(bank):
+            for k in range(pend["n"]):
+                nc.tensor.matmul(out=bank, lhsT=wz[:, 0:P], rhs=wz[:], start=True, stop=True)
+            pend["n"] = 0
+
         gx = const.tile([P, 4096], BF16, name="gx", align_bytes=64)
         xq = const.tile([P, 1024], U32, name="xq", align_bytes=64)
         xs = const.tile([P, 1024], U8, name="xs", align_bytes=64)
@@ -78,6 +94,7 @@ def tile_snn_mlp_kernel(tc, x, w1, w2, out):
             tag = ring["tags"][ring["n"] % len(ring["tags"])]
             ring["n"] += 1
             pt = psum.tile([P, 2, 2, P], F32, name="pt", tag=tag)
+            warm_into(pt[:].rearrange("p s u r -> p (s u r)"))
             for k in range(4):
                 nc.tensor.transpose(pt[:, k // 2, k % 2, :], srcs[k], ident[:])
             d = dst_words.rearrange("p (s r u) -> p s r u", s=2, u=2)
@@ -120,6 +137,7 @@ def tile_snn_mlp_kernel(tc, x, w1, w2, out):
                     fill(srcs, gw_w[:, k * 512 : (k + 1) * 512], "av"[c])
                 if g == 0:
                     q1j(g, j)
+                    warm(WARM_W1[j])
             free_raw(g)
 
         def q1j(g, j):
@@ -138,6 +156,7 @@ def tile_snn_mlp_kernel(tc, x, w1, w2, out):
             gh[g] = gt
             for bc in range(4):
                 hp = psum.tile([P, 4, P], F32, name="hp", tag="mp%d" % bc)
+                warm_into(hp[:].rearrange("p t b -> p (t b)"))
                 for t in range(4):
                     for c in range(2):
                         lo = (t // 2) * 512 + c * 256 + (t % 2) * 128
@@ -209,18 +228,23 @@ def tile_snn_mlp_kernel(tc, x, w1, w2, out):
                     nc.scalar.copy(out=ot[:], in_=po)
                 nc.sync.dma_start(out=out[bt * P : (bt + 1) * P, q * 256 : (q + 1) * 256], in_=ot[:])
 
+        warm(WARM_START)
         t1(0)
         for i in range(4):
             tx(i)
             qx(i)
+            warm(WARM_X[i])
         m1(0)
         t1(1)
         q1(1)
+        warm(WARM_T1[0])
         for g in range(1, G):
             qh(g - 1)
             if g + 1 < G:
                 t1(g + 1)
                 q1(g + 1)
+                if g == 1:
+                    warm(WARM_T1[1])
             else:
                 t2(0, 0, G)
                 q2(0, 0, 4)

@@ -17,10 +17,6 @@ FLOPS = 2 * B * D_IN * D_H + 2 * B * D_H * D_OUT
 G = D_H // 512
 Q = D_OUT // 256
 RAW_BUFS = 8
-WARM_START = 10
-WARM_W1 = (1, 0)
-WARM_X = (1, 0, 1, 1)
-WARM_T1 = (1, 1)
 
 
 def tile_snn_mlp_kernel(tc, x, w1, w2, out):
@@ -70,31 +66,20 @@ def tile_snn_mlp_kernel(tc, x, w1, w2, out):
         nc.vector.memset(scr_a[:], 0.0)
         nc.scalar.activation(out=scr_b[:], in_=scr_a[:], func=RELU)
 
-        wz = const.tile([P, 512], BF16, name="wz")
-        nc.vector.memset(wz[:], 0.0)
-        pend = {"n": 0}
-
-        def warm(n):
-            pend["n"] += n
-
-        def warm_into(bank):
-            for k in range(pend["n"]):
-                nc.tensor.matmul(out=bank, lhsT=wz[:, 0:P], rhs=wz[:], start=True, stop=True)
-            pend["n"] = 0
-
         gx = const.tile([P, 4096], BF16, name="gx", align_bytes=64)
         xq = const.tile([P, 1024], U32, name="xq", align_bytes=64)
         xs = const.tile([P, 1024], U8, name="xs", align_bytes=64)
         hq = const.tile([P, G * 512], U32, name="hq", align_bytes=64)
         hs = const.tile([P, G * 512], U8, name="hs", align_bytes=64)
 
-        ring = {"tags": ["tp0", "tp1", "tp2", "tp3"], "n": 0}
+        ring = {"n": 0}
+
+        def next_bank():
+            ring["n"] += 1
+            return "bank%d" % (ring["n"] % 8)
 
         def fill(srcs, dst_words, eng):
-            tag = ring["tags"][ring["n"] % len(ring["tags"])]
-            ring["n"] += 1
-            pt = psum.tile([P, 2, 2, P], F32, name="pt", tag=tag)
-            warm_into(pt[:].rearrange("p s u r -> p (s u r)"))
+            pt = psum.tile([P, 2, 2, P], F32, name="pt", tag=next_bank())
             for k in range(4):
                 nc.tensor.transpose(pt[:, k // 2, k % 2, :], srcs[k], ident[:])
             d = dst_words.rearrange("p (s r u) -> p s r u", s=2, u=2)
@@ -120,9 +105,9 @@ def tile_snn_mlp_kernel(tc, x, w1, w2, out):
         w1c = {}
 
         def t1(g):
-            gw = stage.tile([P, 4096], BF16, name="gw1", align_bytes=64, bufs=3)
-            cq = stage.tile([P, 1024], U32, name="w1q", align_bytes=64, bufs=3)
-            cs = stage.tile([P, 1024], U8, name="w1s", align_bytes=64, bufs=3)
+            gw = stage.tile([P, 4096], BF16, name="gw1", align_bytes=64, bufs=4)
+            cq = stage.tile([P, 1024], U32, name="w1q", align_bytes=64, bufs=4)
+            cs = stage.tile([P, 1024], U8, name="w1s", align_bytes=64, bufs=4)
             w1c[g] = (gw, cq, cs)
             rw = raw[g][:].bitcast(F32)
             gw_w = gw[:].bitcast(F32)
@@ -137,7 +122,6 @@ def tile_snn_mlp_kernel(tc, x, w1, w2, out):
                     fill(srcs, gw_w[:, k * 512 : (k + 1) * 512], "av"[c])
                 if g == 0:
                     q1j(g, j)
-                    warm(WARM_W1[j])
             free_raw(g)
 
         def q1j(g, j):
@@ -155,8 +139,7 @@ def tile_snn_mlp_kernel(tc, x, w1, w2, out):
             gt = stage.tile([P, 2048], BF16, name="gh", align_bytes=64, bufs=3)
             gh[g] = gt
             for bc in range(4):
-                hp = psum.tile([P, 4, P], F32, name="hp", tag="mp%d" % bc)
-                warm_into(hp[:].rearrange("p t b -> p (t b)"))
+                hp = psum.tile([P, 4, P], F32, name="hp", tag=next_bank())
                 for t in range(4):
                     for c in range(2):
                         lo = (t // 2) * 512 + c * 256 + (t % 2) * 128
@@ -207,13 +190,12 @@ def tile_snn_mlp_kernel(tc, x, w1, w2, out):
 
         def m2(q):
             gw, cq, cs = w2c[q]
-            banks = [psum.tile([P, 2, 256], F32, name="po%d" % k, tag="mp%d" % k) for k in range(2)]
             for bt in range(4):
-                po = banks[bt % 2][:, bt // 2, :]
+                po = psum.tile([P, 256], F32, name="po", tag=next_bank())
                 for g in range(G):
                     lo = g * 512 + bt * 128
                     nc.tensor.matmul_mx(
-                        out=po,
+                        out=po[:],
                         lhsT=hq[:, lo : lo + 128].bitcast(FP8X4),
                         lhsT_scale=hs[:, lo : lo + 128],
                         rhs=cq[:, g * 256 : (g + 1) * 256].bitcast(FP8X4),
@@ -223,36 +205,46 @@ def tile_snn_mlp_kernel(tc, x, w1, w2, out):
                     )
                 ot = stage.tile([P, 256], F32, name="ot", bufs=4)
                 if q == Q - 1 and bt % 2 == 1:
-                    nc.vector.tensor_copy(out=ot[:], in_=po)
+                    nc.vector.tensor_copy(out=ot[:], in_=po[:])
                 else:
-                    nc.scalar.copy(out=ot[:], in_=po)
+                    nc.scalar.copy(out=ot[:], in_=po[:])
                 nc.sync.dma_start(out=out[bt * P : (bt + 1) * P, q * 256 : (q + 1) * 256], in_=ot[:])
 
-        warm(WARM_START)
         t1(0)
         for i in range(4):
             tx(i)
             qx(i)
-            warm(WARM_X[i])
         m1(0)
         t1(1)
         q1(1)
-        warm(WARM_T1[0])
-        for g in range(1, G):
-            qh(g - 1)
-            if g + 1 < G:
-                t1(g + 1)
-                q1(g + 1)
-                if g == 1:
-                    warm(WARM_T1[1])
-            else:
-                t2(0, 0, G)
-                q2(0, 0, 4)
+        t1(2)
+        q1(2)
+        m1(1)
+        qh(0)
+        for g in (2, 4):
+            t1(g + 1)
+            q1(g + 1)
+            t1(g + 2)
+            q1(g + 2)
             m1(g)
-        ring["tags"] = ["tp0", "tp1", "tp2", "tp3", "mp2", "mp3"]
-        qh(G - 1)
+            qh(g - 1)
+            m1(g + 1)
+            qh(g)
+        t1(7)
+        q1(7)
+        t2(0, 0, 4)
+        q2(0, 0, 2)
+        m1(6)
+        qh(5)
+        m1(7)
+        qh(6)
+        t2(0, 4, 8)
+        q2(0, 2, 4)
         for q in range(Q):
             if q + 1 < Q:
-                t2(q + 1, 0, G)
+                t2(q + 1, 0, 2)
+                if q == 0:
+                    qh(G - 1)
+                t2(q + 1, 2, 8)
                 q2(q + 1, 0, 4)
             m2(q)

@@ -105,7 +105,7 @@ def tile_snn_mlp_kernel(tc, x, w1, w2, out):
         w1c = {}
 
         def t1(g):
-            gw = stage.tile([P, 4096], BF16, name="gw1", align_bytes=64, bufs=4)
+            gw = stage.tile([P, 4096], BF16, name="gw1", align_bytes=64, bufs=3)
             cq = stage.tile([P, 1024], U32, name="w1q", align_bytes=64, bufs=4)
             cs = stage.tile([P, 1024], U8, name="w1s", align_bytes=64, bufs=4)
             w1c[g] = (gw, cq, cs)
@@ -168,8 +168,8 @@ def tile_snn_mlp_kernel(tc, x, w1, w2, out):
         def t2(q, g_lo, g_hi):
             if g_lo == 0:
                 gw = stage.tile([P, 8192], BF16, name="gw2", align_bytes=64)
-                cq = stage.tile([P, 2048], U32, name="w2q", align_bytes=64)
-                cs = stage.tile([P, 2048], U8, name="w2s", align_bytes=64)
+                cq = stage.tile([P, 2048], U32, name="w2q", align_bytes=64, bufs=3)
+                cs = stage.tile([P, 2048], U8, name="w2s", align_bytes=64, bufs=3)
                 w2c[q] = (gw, cq, cs)
             gw_w = w2c[q][0][:].bitcast(F32)
             for g in range(g_lo, g_hi):
@@ -240,11 +240,15 @@ def tile_snn_mlp_kernel(tc, x, w1, w2, out):
         qh(6)
         t2(0, 4, 8)
         q2(0, 2, 4)
-        for q in range(Q):
-            if q + 1 < Q:
-                t2(q + 1, 0, 2)
-                if q == 0:
-                    qh(G - 1)
-                t2(q + 1, 2, 8)
-                q2(q + 1, 0, 4)
-            m2(q)
+        t2(1, 0, 2)
+        qh(G - 1)
+        t2(1, 2, 8)
+        q2(1, 0, 4)
+        m2(0)
+        t2(2, 0, 8)
+        t2(3, 0, 8)
+        q2(2, 0, 4)
+        q2(3, 0, 4)
+        m2(1)
+        m2(2)
+        m2(3)

@@ -26,7 +26,6 @@ def tile_snn_mlp_kernel(tc, x, w1, w2, out):
         rawp = ctx.enter_context(tc.tile_pool(name="rawp", bufs=1))
         stage = ctx.enter_context(tc.tile_pool(name="stage", bufs=2))
         psum = ctx.enter_context(tc.psum_pool(name="psum", bufs=1))
-        ctx.enter_context(tc.manual_schedule())
 
         w1_v = w1.rearrange("(g j p e) k -> g p j e k", g=G, j=2, p=P, e=2)
         w2_v = w2.rearrange("(i p) k -> i p k", p=P)

from contextlib import ExitStack

import concourse.mybir as mybir
from concourse.masks import make_identity

F32 = mybir.dt.float32
BF16 = mybir.dt.bfloat16
U32 = mybir.dt.uint32
U8 = mybir.dt.uint8
FP8X4 = mybir.dt.float8_e4m3fn_x4
RELU = mybir.ActivationFunctionType.Relu

P = 128
B, D_IN, D_H, D_OUT = 512, 1024, 4096, 1024
FLOPS = 2 * B * D_IN * D_H + 2 * B * D_H * D_OUT

G = D_H // 512
Q = D_OUT // 256
RAW_BUFS = 8


def tile_snn_mlp_kernel(tc, x, w1, w2, out):
    nc = tc.nc
    with ExitStack() as ctx:
        const = ctx.enter_context(tc.tile_pool(name="const", bufs=1))
        rawp = ctx.enter_context(tc.tile_pool(name="rawp", bufs=1))
        stage = ctx.enter_context(tc.tile_pool(name="stage", bufs=2))
        psum = ctx.enter_context(tc.psum_pool(name="psum", bufs=1))

        w1_v = w1.rearrange("(g j p e) k -> g p j e k", g=G, j=2, p=P, e=2)
        w2_v = w2.rearrange("(i p) k -> i p k", p=P)

        raw = {}

        def load_raw(n):
            t = rawp.tile([P, 4096], BF16, name="raw%d" % n, tag="slot%d" % (n % RAW_BUFS))
            raw[n] = t
            if n == 0:
                tv = t[:].rearrange("p (j e k) -> p j e k", j=2, e=2)
                for j in range(2):
                    nc.sync.dma_start(out=tv[:, j], in_=w1_v[0][:, j])
            elif n < G:
                nc.sync.dma_start(out=t[:].rearrange("p (j e k) -> p j e k", j=2, e=2), in_=w1_v[n])
            else:
                nc.sync.dma_start(out=t[:], in_=w2_v[n - G])

        def free_raw(n):
            if n + RAW_BUFS < 2 * G:
                load_raw(n + RAW_BUFS)

        load_raw(0)
        xr = []
        for i in range(4):
            t = const.tile([P, D_IN], BF16, name="xr%d" % i)
            nc.sync.dma_start(out=t[:], in_=x[i * P : (i + 1) * P, :])
            xr.append(t)
        for n in range(1, RAW_BUFS):
            load_raw(n)

        ident = const.tile([P, P], F32, name="ident")
        make_identity(nc, ident[:])

        scr_a = const.tile([P, 1], F32, name="scr_a")
        scr_b = const.tile([P, 1], F32, name="scr_b")
        nc.vector.memset(scr_a[:], 0.0)
        nc.scalar.activation(out=scr_b[:], in_=scr_a[:], func=RELU)

        gx = const.tile([P, 4096], BF16, name="gx", align_bytes=64)
        xq = const.tile([P, 1024], U32, name="xq", align_bytes=64)
        xs = const.tile([P, 1024], U8, name="xs", align_bytes=64)
        hq = const.tile([P, G * 512], U32, name="hq", align_bytes=64)
        hs = const.tile([P, G * 512], U8, name="hs", align_bytes=64)

        ring = {"n": 0}

        def next_bank():
            ring["n"] += 1
            return "bank%d" % (ring["n"] % 8)

        def fill(srcs, dst_words, eng):
            pt = psum.tile([P, 2, 2, P], F32, name="pt", tag=next_bank())
            for k in range(4):
                nc.tensor.transpose(pt[:, k // 2, k % 2, :], srcs[k], ident[:])
            d = dst_words.rearrange("p (s r u) -> p s r u", s=2, u=2)
            s = pt[:].rearrange("p s u r -> p s r u")
            if eng == "v":
                nc.vector.tensor_copy(out=d, in_=s)
            else:
                nc.scalar.copy(out=d, in_=s)

        def quant(codes, scales, src):
            nc.vector.quantize_mx(out=codes.bitcast(FP8X4), scales=scales, in_=src)

        gx_w = gx[:].bitcast(F32)

        def tx(i):
            xw = xr[i][:].bitcast(F32)
            srcs = [xw[:, 256 * c + 128 * u : 256 * c + 128 * u + 128] for c in range(2) for u in range(2)]
            fill(srcs, gx_w[:, i * 512 : (i + 1) * 512], "a")

        def qx(i):
            quant(xq[:, i * 256 : (i + 1) * 256], xs[:, i * 256 : (i + 1) * 256], gx[:, i * 1024 : (i + 1) * 1024])

        w1c = {}

        def t1(g):
            gw = stage.tile([P, 4096], BF16, name="gw1", align_bytes=64, bufs=3)
            cq = stage.tile([P, 1024], U32, name="w1q", align_bytes=64, bufs=4)
            cs = stage.tile([P, 1024], U8, name="w1s", align_bytes=64, bufs=4)
            w1c[g] = (gw, cq, cs)
            rw = raw[g][:].bitcast(F32)
            gw_w = gw[:].bitcast(F32)
            for j in range(2):
                for c in range(2):
                    srcs = [
                        rw[:, j * 1024 + e * 512 + 256 * c + 128 * u : j * 1024 + e * 512 + 256 * c + 128 * u + 128]
                        for e in range(2)
                        for u in range(2)
                    ]
                    k = j * 2 + c
                    fill(srcs, gw_w[:, k * 512 : (k + 1) * 512], "av"[c])
                if g == 0:
                    q1j(g, j)
            free_raw(g)

        def q1j(g, j):
            gw, cq, cs = w1c[g]
            quant(cq[:, j * 512 : (j + 1) * 512], cs[:, j * 512 : (j + 1) * 512], gw[:, j * 2048 : (j + 1) * 2048])

        def q1(g):
            for j in range(2):
                q1j(g, j)

        gh = {}

        def m1(g):
            gw, cq, cs = w1c[g]
            gt = stage.tile([P, 2048], BF16, name="gh", align_bytes=64, bufs=3)
            gh[g] = gt
            for bc in range(4):
                hp = psum.tile([P, 4, P], F32, name="hp", tag=next_bank())
                for t in range(4):
                    for c in range(2):
                        lo = (t // 2) * 512 + c * 256 + (t % 2) * 128
                        ro = bc * 256 + c * 128
                        nc.tensor.matmul_mx(
                            out=hp[:, t, :],
                            lhsT=cq[:, lo : lo + 128].bitcast(FP8X4),
                            lhsT_scale=cs[:, lo : lo + 128],
                            rhs=xq[:, ro : ro + 128].bitcast(FP8X4),
                            rhs_scale=xs[:, ro : ro + 128],
                            start=(c == 0),
                            stop=(c == 1),
                        )
                d = gt[:, bc * 512 : (bc + 1) * 512].rearrange("p (b t) -> p b t", t=4)
                s = hp[:].rearrange("p t b -> p b t")
                if bc == 3 and g % 2 == 0:
                    nc.vector.tensor_scalar_max(out=d, in0=s, scalar1=0.0)
                else:
                    nc.scalar.activation(out=d, in_=s, func=RELU)

        def qh(g):
            quant(hq[:, g * 512 : (g + 1) * 512], hs[:, g * 512 : (g + 1) * 512], gh[g][:])

        w2c = {}

        def t2(q, g_lo, g_hi):
            if g_lo == 0:
                gw = stage.tile([P, 8192], BF16, name="gw2", align_bytes=64)
                cq = stage.tile([P, 2048], U32, name="w2q", align_bytes=64, bufs=3)
                cs = stage.tile([P, 2048], U8, name="w2s", align_bytes=64, bufs=3)
                w2c[q] = (gw, cq, cs)
            gw_w = w2c[q][0][:].bitcast(F32)
            for g in range(g_lo, g_hi):
                srcs = [
                    raw[G + 2 * q + s][:].bitcast(F32)[:, 256 * g + 128 * u : 256 * g + 128 * u + 128]
                    for s in range(2)
                    for u in range(2)
                ]
                fill(srcs, gw_w[:, g * 512 : (g + 1) * 512], "av"[g % 2])
            if g_hi == G:
                free_raw(G + 2 * q)
                free_raw(G + 2 * q + 1)

        def q2(q, k_lo, k_hi):
            gw, cq, cs = w2c[q]
            for k in range(k_lo, k_hi):
                quant(cq[:, k * 512 : (k + 1) * 512], cs[:, k * 512 : (k + 1) * 512], gw[:, k * 2048 : (k + 1) * 2048])

        def m2(q):
            gw, cq, cs = w2c[q]
            for bt in range(4):
                po = psum.tile([P, 256], F32, name="po", tag=next_bank())
                for g in range(G):
                    lo = g * 512 + bt * 128
                    nc.tensor.matmul_mx(
                        out=po[:],
                        lhsT=hq[:, lo : lo + 128].bitcast(FP8X4),
                        lhsT_scale=hs[:, lo : lo + 128],
                        rhs=cq[:, g * 256 : (g + 1) * 256].bitcast(FP8X4),
                        rhs_scale=cs[:, g * 256 : (g + 1) * 256],
                        start=(g == 0),
                        stop=(g == G - 1),
                    )
                ot = stage.tile([P, 256], F32, name="ot", bufs=4)
                if q == Q - 1 and bt % 2 == 1:
                    nc.vector.tensor_copy(out=ot[:], in_=po[:])
                else:
                    nc.scalar.copy(out=ot[:], in_=po[:])
                nc.sync.dma_start(out=out[bt * P : (bt + 1) * P, q * 256 : (q + 1) * 256], in_=ot[:])

        t1(0)
        for i in range(4):
            tx(i)
            qx(i)
        m1(0)
        t1(1)
        q1(1)
        t1(2)
        q1(2)
        m1(1)
        qh(0)
        for g in (2, 4):
            t1(g + 1)
            q1(g + 1)
            t1(g + 2)
            q1(g + 2)
            m1(g)
            qh(g - 1)
            m1(g + 1)
            qh(g)
        t1(7)
        q1(7)
        t2(0, 0, 4)
        q2(0, 0, 2)
        m1(6)
        qh(5)
        m1(7)
        qh(6)
        t2(0, 4, 8)
        q2(0, 2, 4)
        t2(1, 0, 2)
        qh(G - 1)
        t2(1, 2, 8)
        q2(1, 0, 4)
        m2(0)
        t2(2, 0, 8)
        t2(3, 0, 8)
        q2(2, 0, 4)
        q2(3, 0, 4)
        m2(1)
        m2(2)
        m2(3)
